import numpy as np
import ml_dtypes


def mxq(x, axis, fmt="e4m3"):
    dtype, down = {"e4m3": (ml_dtypes.float8_e4m3fn, 7), "e5m2": (ml_dtypes.float8_e5m2, 14)}[fmt]
    v = np.moveaxis(np.asarray(x, np.float32).astype(ml_dtypes.bfloat16).astype(np.float64), axis, -1)
    blocks = v.reshape(v.shape[:-1] + (-1, 32))
    amax = np.abs(blocks).max(-1, keepdims=True)
    byte = np.maximum(np.where(amax > 0, np.frexp(amax)[1] - 1 + 127, 0) - down, 1)
    scale = np.exp2(byte - 127.0)
    codes = (blocks / scale).astype(np.float32).astype(dtype).astype(np.float64)
    return np.moveaxis((codes * scale).reshape(v.shape), -1, axis)


WIDE = False


def mx_kscale(k):
    if not WIDE:
        return np.ones(k)
    levels = np.array([10, -10, 5, -5, 0])
    a = np.random.permutation(np.resize(levels, k // 512 * 4)).reshape(k // 512, 4)
    idx = np.arange(k)
    return np.exp2(a[idx // 512, idx % 128 // 32])


BF16 = ml_dtypes.bfloat16


def bf(x):
    return np.asarray(x, np.float32).astype(BF16)


def f64(x):
    return np.asarray(x).astype(np.float64)


B, L, D, DK = 16, 512, 256, 128


def setup_inputs():
    s = mx_kscale(L)
    return {"energy": bf(np.random.standard_normal((B, L, L)) * 0.25 * np.sqrt(DK) * s),
            "Wl1": bf(np.random.standard_normal((L, L)) * 0.7 / np.sqrt(L) / s),
            "bl1": bf(np.random.standard_normal(L) * 0.5),
            "v2": bf(np.random.standard_normal((B, L, D)) * 2.0),
            "gamma1": bf(1.0 + 0.1 * np.random.standard_normal(1)),
            "x": bf(np.random.standard_normal((B, L, D)))}


def reference(energy, Wl1, bl1, v2, gamma1, x):
    z = (mxq(f64(energy), 2, "e4m3") @ mxq(f64(Wl1).T, 0, "e4m3")) + f64(bl1)
    e = np.exp(z - z.max(-1, keepdims=True))
    att1 = e / e.sum(-1, keepdims=True)
    o = mxq(f64(v2).transpose(0, 2, 1), 2, "e4m3") @ mxq(att1, 1, "e4m3")
    return f64(gamma1) * o.reshape(B, L, D) + f64(x)

@@ -1,0 +1,202 @@
+from contextlib import ExitStack
+
+from concourse import mybir
+from concourse.masks import make_identity
+
+F32 = mybir.dt.float32
+BF16 = mybir.dt.bfloat16
+U32 = mybir.dt.uint32
+U8 = mybir.dt.uint8
+FP8X4 = mybir.dt.float8_e4m3fn_x4
+ALU = mybir.AluOpType
+ACT = mybir.ActivationFunctionType
+
+B, L, D = 16, 512, 256
+P = 128
+PACK = 4
+L_TILES = L // P
+D_TILES = D // P
+WORDS = L // 2
+
+FLOPS = B * (2 * L * L * L + 2 * D * L * L)
+
+
+def k_onto_partitions(nc, psum, identity, rows, grouped):
+    row_words = rows.bitcast(F32)
+    grouped_words = grouped.bitcast(F32).rearrange("q (c u) -> q c u", u=2)
+    for half in range(2):
+        turned = psum.tile([P, 2, 2 * P], F32, tag="turned%d" % half)
+        for i in range(2):
+            for u in range(2):
+                nc.tensor.transpose(
+                    turned[:, u, i * P : (i + 1) * P],
+                    row_words[:, 2 * half + i, u * P : (u + 1) * P],
+                    identity,
+                )
+        nc.scalar.copy(
+            out=grouped_words[:, half * 2 * P : (half + 1) * 2 * P, :],
+            in_=turned[:].rearrange("q u c -> q c u"),
+        )
+
+
+def tile_dualcrossmodalattention_pa_t_kernel(tc, energy, Wl1, bl1, v2, gamma1, x, out):
+    nc = tc.nc
+    with ExitStack() as ctx:
+        ctx.enter_context(tc.manual_schedule())
+        const = ctx.enter_context(tc.tile_pool(name="const", bufs=1))
+        inputs = ctx.enter_context(tc.tile_pool(name="inputs", bufs=B))
+        work = ctx.enter_context(tc.tile_pool(name="work", bufs=2))
+        held = ctx.enter_context(tc.tile_pool(name="held", bufs=4))
+        psum = ctx.enter_context(tc.psum_pool(name="psum", bufs=1))
+
+        w_rows = const.tile([P, L_TILES, L], BF16)
+        nc.sync.dma_start(out=w_rows[:], in_=Wl1.rearrange("(j p) k -> p j k", p=P))
+        bias = const.tile([P, L], BF16)
+        nc.scalar.dma_start(out=bias[:], in_=bl1.partition_broadcast(P))
+        gamma_bf = const.tile([P, 1], BF16)
+        nc.scalar.dma_start(out=gamma_bf[:], in_=gamma1.partition_broadcast(P))
+
+        energy_rows, v2_rows, x_rows = [], [], []
+        for b in range(B):
+            e_in = inputs.tile([P, PACK, L], BF16, tag="energy")
+            nc.sync.dma_start(out=e_in[:], in_=energy[b].rearrange("(p t) k -> p t k", t=PACK))
+            energy_rows.append(e_in)
+            v_in = inputs.tile([P, PACK, D], BF16, tag="v2")
+            nc.sync.dma_start(out=v_in[:], in_=v2[b].rearrange("(p t) d -> p t d", t=PACK))
+            v2_rows.append(v_in)
+            x_in = inputs.tile([P, D_TILES, L], BF16, tag="x")
+            nc.sync.dma_start(out=x_in[:], in_=x[b].rearrange("(i p h) j -> p i (h j)", i=D_TILES, h=2))
+            x_rows.append(x_in)
+
+        identity = const.tile([P, P], F32)
+        make_identity(nc, identity[:])
+
+        w_grouped = const.tile([P, PACK * L], BF16, align_bytes=64)
+        k_onto_partitions(nc, psum, identity[:], w_rows[:], w_grouped[:])
+        w_codes = const.tile([P, L], U32, align_bytes=64)
+        w_scales = const.tile([P, L], U8, align_bytes=64)
+        nc.vector.quantize_mx(out=w_codes[:].bitcast(FP8X4), scales=w_scales[:], in_=w_grouped[:])
+        gamma = const.tile([P, 1], F32)
+        nc.vector.tensor_copy(out=gamma[:], in_=gamma_bf[:])
+
+        e_grouped, v_grouped, v_mx, z_banks = {}, {}, {}, {}
+        logits, neg_max, att_grouped, o_banks = {}, {}, {}, {}
+
+        def regroup_inputs(b):
+            e_group = work.tile([P, PACK * L], BF16, align_bytes=64)
+            k_onto_partitions(nc, psum, identity[:], energy_rows[b][:], e_group[:])
+            e_grouped[b] = e_group
+            v_group = work.tile([P, D, PACK], BF16, align_bytes=64)
+            nc.scalar.copy(
+                out=v_group[:].rearrange("p (c i) t -> p c t i", i=4),
+                in_=v2_rows[b][:].rearrange("p t (c i) -> p c t i", i=4),
+            )
+            v_grouped[b] = v_group
+
+        def first_matmul(b):
+            e_codes = work.tile([P, L], U32, align_bytes=64)
+            e_scales = work.tile([P, L], U8, align_bytes=64)
+            nc.vector.quantize_mx(out=e_codes[:].bitcast(FP8X4), scales=e_scales[:], in_=e_grouped[b][:])
+            v_codes = held.tile([P, D], U32, align_bytes=64)
+            v_scales = held.tile([P, D], U8, align_bytes=64)
+            nc.vector.quantize_mx(
+                out=v_codes[:].bitcast(FP8X4),
+                scales=v_scales[:],
+                in_=v_grouped[b][:].rearrange("p d t -> p (d t)"),
+            )
+            v_mx[b] = (v_codes, v_scales)
+            z_banks[b] = []
+            for t in range(L_TILES):
+                z = psum.tile([P, L], F32, tag="z%d" % t)
+                nc.tensor.matmul_mx(
+                    out=z[:],
+                    lhsT=e_codes[:, t * P : (t + 1) * P].bitcast(FP8X4),
+                    lhsT_scale=e_scales[:, t * P : (t + 1) * P],
+                    rhs=w_codes[:].bitcast(FP8X4),
+                    rhs_scale=w_scales[:],
+                    start=True,
+                    stop=True,
+                )
+                z_banks[b].append(z)
+
+        def bias_and_max(b):
+            logit = work.tile([P, L_TILES, L], F32, bufs=3)
+            for t in range(L_TILES):
+                nc.vector.tensor_tensor(out=logit[:, t, :], in0=z_banks[b][t][:], in1=bias[:], op=ALU.add)
+            minus_max = work.tile([P, L_TILES], F32, bufs=3)
+            nc.vector.tensor_reduce(
+                out=minus_max[:], in_=logit[:], axis=mybir.AxisListType.X, op=ALU.max, negate=True
+            )
+            logits[b], neg_max[b] = logit, minus_max
+
+        def softmax(b):
+            row_sum = work.tile([P, L_TILES], F32, bufs=3)
+            for t in range(L_TILES):
+                nc.scalar.activation(
+                    out=logits[b][:, t, :],
+                    in_=logits[b][:, t, :],
+                    func=ACT.Exp,
+                    bias=neg_max[b][:, t : t + 1],
+                    scale=1.0,
+                    accum_out=row_sum[:, t : t + 1],
+                )
+            inv_sum = work.tile([P, L_TILES], F32, bufs=3)
+            nc.vector.reciprocal(out=inv_sum[:], in_=row_sum[:])
+            att_group = work.tile([P, L, PACK], BF16, align_bytes=64)
+            nc.gpsimd.tensor_tensor(
+                out=att_group[:],
+                in0=logits[b][:].rearrange("p t m -> p m t"),
+                in1=inv_sum[:].unsqueeze(1).to_broadcast([P, L, PACK]),
+                op=ALU.mult,
+            )
+            att_grouped[b] = att_group
+
+        def second_matmul(b):
+            att_codes = work.tile([P, L], U32, align_bytes=64)
+            att_scales = work.tile([P, L], U8, align_bytes=64)
+            nc.vector.quantize_mx(
+                out=att_codes[:].bitcast(FP8X4),
+                scales=att_scales[:],
+                in_=att_grouped[b][:].rearrange("p m t -> p (m t)"),
+            )
+            v_codes, v_scales = v_mx[b]
+            o_banks[b] = []
+            for i in range(D_TILES):
+                o = psum.tile([P, L], F32, tag="o%d" % i)
+                nc.tensor.matmul_mx(
+                    out=o[:],
+                    lhsT=v_codes[:, i * P : (i + 1) * P].bitcast(FP8X4),
+                    lhsT_scale=v_scales[:, i * P : (i + 1) * P],
+                    rhs=att_codes[:].bitcast(FP8X4),
+                    rhs_scale=att_scales[:],
+                    start=True,
+                    stop=True,
+                )
+                o_banks[b].append(o)
+
+        def gain_and_residual(b):
+            result = work.tile([P, D_TILES, L], F32, bufs=3)
+            for i in range(D_TILES):
+                nc.vector.scalar_tensor_tensor(
+                    out=result[:, i, :],
+                    in0=o_banks[b][i][:],
+                    scalar=gamma[:, 0:1],
+                    in1=x_rows[b][:, i, :],
+                    op0=ALU.mult,
+                    op1=ALU.add,
+                )
+            nc.sync.dma_start(
+                out=out[b].rearrange("(i p h) j -> p i (h j)", i=D_TILES, h=2), in_=result[:]
+            )
+
+        def if_sample(stage, b):
+            if 0 <= b < B:
+                stage(b)
+
+        for s in range(-2, B + 2):
+            if_sample(bias_and_max, s)
+            if_sample(gain_and_residual, s - 2)
+            if_sample(regroup_inputs, s + 2)
+            if_sample(first_matmul, s + 1)
+            if_sample(second_matmul, s - 1)
+            if_sample(softmax, s)

@@ -16,7 +16,6 @@ P = 128
 PACK = 4
 L_TILES = L // P
 D_TILES = D // P
-WORDS = L // 2
 
 FLOPS = B * (2 * L * L * L + 2 * D * L * L)
 
@@ -24,17 +23,17 @@ FLOPS = B * (2 * L * L * L + 2 * D * L * L)
 def k_onto_partitions(nc, psum, identity, rows, grouped):
     row_words = rows.bitcast(F32)
     grouped_words = grouped.bitcast(F32).rearrange("q (c u) -> q c u", u=2)
-    for half in range(2):
-        turned = psum.tile([P, 2, 2 * P], F32, tag="turned%d" % half)
+    for bank in range(2):
+        turned = psum.tile([P, 2, 2 * P], F32, tag="turned%d" % bank)
         for i in range(2):
             for u in range(2):
                 nc.tensor.transpose(
                     turned[:, u, i * P : (i + 1) * P],
-                    row_words[:, 2 * half + i, u * P : (u + 1) * P],
+                    row_words[:, 2 * bank + i, u * P : (u + 1) * P],
                     identity,
                 )
-        nc.scalar.copy(
-            out=grouped_words[:, half * 2 * P : (half + 1) * 2 * P, :],
+        nc.vector.tensor_copy(
+            out=grouped_words[:, bank * 2 * P : (bank + 1) * 2 * P, :],
             in_=turned[:].rearrange("q u c -> q c u"),
         )
 
@@ -46,13 +45,14 @@ def tile_dualcrossmodalattention_pa_t_kernel(tc, energy, Wl1, bl1, v2, gamma1, x
         const = ctx.enter_context(tc.tile_pool(name="const", bufs=1))
         inputs = ctx.enter_context(tc.tile_pool(name="inputs", bufs=B))
         work = ctx.enter_context(tc.tile_pool(name="work", bufs=2))
-        held = ctx.enter_context(tc.tile_pool(name="held", bufs=4))
+        held = ctx.enter_context(tc.tile_pool(name="held", bufs=6))
         psum = ctx.enter_context(tc.psum_pool(name="psum", bufs=1))
 
         w_rows = const.tile([P, L_TILES, L], BF16)
         nc.sync.dma_start(out=w_rows[:], in_=Wl1.rearrange("(j p) k -> p j k", p=P))
-        bias = const.tile([P, L], BF16)
-        nc.scalar.dma_start(out=bias[:], in_=bl1.partition_broadcast(P))
+        bias_rows_bf = const.tile([P, P], BF16)
+        nc.vector.memset(bias_rows_bf[:], 0.0)
+        nc.scalar.dma_start(out=bias_rows_bf[0:L_TILES, :], in_=bl1.rearrange("(j p) -> j p", p=P))
         gamma_bf = const.tile([P, 1], BF16)
         nc.scalar.dma_start(out=gamma_bf[:], in_=gamma1.partition_broadcast(P))
 
@@ -76,16 +76,25 @@ def tile_dualcrossmodalattention_pa_t_kernel(tc, energy, Wl1, bl1, v2, gamma1, x
         w_codes = const.tile([P, L], U32, align_bytes=64)
         w_scales = const.tile([P, L], U8, align_bytes=64)
         nc.vector.quantize_mx(out=w_codes[:].bitcast(FP8X4), scales=w_scales[:], in_=w_grouped[:])
+
+        bias_rows = const.tile([P, P], F32)
+        nc.vector.tensor_copy(out=bias_rows[:], in_=bias_rows_bf[:])
+        bias_turned = psum.tile([P, P], F32, tag="o0")
+        nc.tensor.transpose(bias_turned[:], bias_rows[:], identity[:])
+        bias_col = const.tile([P, L_TILES], F32)
+        nc.vector.tensor_copy(out=bias_col[:], in_=bias_turned[:, 0:L_TILES])
         gamma = const.tile([P, 1], F32)
         nc.vector.tensor_copy(out=gamma[:], in_=gamma_bf[:])
 
-        e_grouped, v_grouped, v_mx, z_banks = {}, {}, {}, {}
-        logits, neg_max, att_grouped, o_banks = {}, {}, {}, {}
+        e_grouped, v_grouped, e_mx, v_mx, z_banks, logits = {}, {}, {}, {}, {}, {}
+        neg_max, row_sum, exps, att_grouped, att_mx, o_banks = {}, {}, {}, {}, {}, {}
 
-        def regroup_inputs(b):
+        def regroup_energy(b):
             e_group = work.tile([P, PACK * L], BF16, align_bytes=64)
             k_onto_partitions(nc, psum, identity[:], energy_rows[b][:], e_group[:])
             e_grouped[b] = e_group
+
+        def regroup_v2(b):
             v_group = work.tile([P, D, PACK], BF16, align_bytes=64)
             nc.scalar.copy(
                 out=v_group[:].rearrange("p (c i) t -> p c t i", i=4),
@@ -93,10 +102,11 @@ def tile_dualcrossmodalattention_pa_t_kernel(tc, energy, Wl1, bl1, v2, gamma1, x
             )
             v_grouped[b] = v_group
 
-        def first_matmul(b):
-            e_codes = work.tile([P, L], U32, align_bytes=64)
-            e_scales = work.tile([P, L], U8, align_bytes=64)
+        def quantise_inputs(b):
+            e_codes = work.tile([P, L], U32, align_bytes=64, bufs=3)
+            e_scales = work.tile([P, L], U8, align_bytes=64, bufs=3)
             nc.vector.quantize_mx(out=e_codes[:].bitcast(FP8X4), scales=e_scales[:], in_=e_grouped[b][:])
+            e_mx[b] = (e_codes, e_scales)
             v_codes = held.tile([P, D], U32, align_bytes=64)
             v_scales = held.tile([P, D], U8, align_bytes=64)
             nc.vector.quantize_mx(
@@ -105,53 +115,76 @@ def tile_dualcrossmodalattention_pa_t_kernel(tc, energy, Wl1, bl1, v2, gamma1, x
                 in_=v_grouped[b][:].rearrange("p d t -> p (d t)"),
             )
             v_mx[b] = (v_codes, v_scales)
-            z_banks[b] = []
-            for t in range(L_TILES):
-                z = psum.tile([P, L], F32, tag="z%d" % t)
+
+        def first_matmul(b, half):
+            e_codes, e_scales = e_mx[b]
+            for j in (2 * half, 2 * half + 1):
+                z = psum.tile([P, L], F32, tag="z%d" % (j % 2))
                 nc.tensor.matmul_mx(
                     out=z[:],
-                    lhsT=e_codes[:, t * P : (t + 1) * P].bitcast(FP8X4),
-                    lhsT_scale=e_scales[:, t * P : (t + 1) * P],
-                    rhs=w_codes[:].bitcast(FP8X4),
-                    rhs_scale=w_scales[:],
+                    lhsT=w_codes[:, j * P : (j + 1) * P].bitcast(FP8X4),
+                    lhsT_scale=w_scales[:, j * P : (j + 1) * P],
+                    rhs=e_codes[:].bitcast(FP8X4),
+                    rhs_scale=e_scales[:],
                     start=True,
                     stop=True,
                 )
-                z_banks[b].append(z)
+                z_banks[b, j] = z
 
-        def bias_and_max(b):
-            logit = work.tile([P, L_TILES, L], F32, bufs=3)
-            for t in range(L_TILES):
-                nc.vector.tensor_tensor(out=logit[:, t, :], in0=z_banks[b][t][:], in1=bias[:], op=ALU.add)
-            minus_max = work.tile([P, L_TILES], F32, bufs=3)
-            nc.vector.tensor_reduce(
-                out=minus_max[:], in_=logit[:], axis=mybir.AxisListType.X, op=ALU.max, negate=True
-            )
-            logits[b], neg_max[b] = logit, minus_max
-
-        def softmax(b):
-            row_sum = work.tile([P, L_TILES], F32, bufs=3)
-            for t in range(L_TILES):
+        def add_bias(b, half):
+            if half == 0:
+                logit = work.tile([P, L_TILES, L], F32)
+                logits[b] = logit
+            for j in (2 * half, 2 * half + 1):
                 nc.scalar.activation(
-                    out=logits[b][:, t, :],
-                    in_=logits[b][:, t, :],
+                    out=logits[b][:, j, :],
+                    in_=z_banks[b, j][:],
+                    func=ACT.Identity,
+                    bias=bias_col[:, j : j + 1],
+                    scale=1.0,
+                )
+
+        def softmax_rows(b, half):
+            if half == 0:
+                minus_max = work.tile([P, L_TILES], F32, bufs=3)
+                sums = work.tile([P, L_TILES], F32, bufs=3)
+                exp_tile = work.tile([P, L_TILES, L], F32)
+                neg_max[b], row_sum[b], exps[b] = minus_max, sums, exp_tile
+            for t in (2 * half, 2 * half + 1):
+                rows = psum.tile([P, L], F32, tag="rows%d" % (t % 2))
+                for j in range(L_TILES):
+                    nc.tensor.transpose(
+                        rows[:, j * P : (j + 1) * P], logits[b][:, j, t * P : (t + 1) * P], identity[:]
+                    )
+                nc.vector.tensor_reduce(
+                    out=neg_max[b][:, t : t + 1],
+                    in_=rows[:],
+                    axis=mybir.AxisListType.X,
+                    op=ALU.max,
+                    negate=True,
+                )
+                nc.scalar.activation(
+                    out=exps[b][:, t, :],
+                    in_=rows[:],
                     func=ACT.Exp,
                     bias=neg_max[b][:, t : t + 1],
                     scale=1.0,
-                    accum_out=row_sum[:, t : t + 1],
+                    accum_out=row_sum[b][:, t : t + 1],
                 )
+
+        def normalise(b):
             inv_sum = work.tile([P, L_TILES], F32, bufs=3)
-            nc.vector.reciprocal(out=inv_sum[:], in_=row_sum[:])
+            nc.vector.reciprocal(out=inv_sum[:], in_=row_sum[b][:])
             att_group = work.tile([P, L, PACK], BF16, align_bytes=64)
             nc.gpsimd.tensor_tensor(
                 out=att_group[:],
-                in0=logits[b][:].rearrange("p t m -> p m t"),
+                in0=exps[b][:].rearrange("p t m -> p m t"),
                 in1=inv_sum[:].unsqueeze(1).to_broadcast([P, L, PACK]),
                 op=ALU.mult,
             )
             att_grouped[b] = att_group
 
-        def second_matmul(b):
+        def quantise_att(b):
             att_codes = work.tile([P, L], U32, align_bytes=64)
             att_scales = work.tile([P, L], U8, align_bytes=64)
             nc.vector.quantize_mx(
@@ -159,8 +192,11 @@ def tile_dualcrossmodalattention_pa_t_kernel(tc, energy, Wl1, bl1, v2, gamma1, x
                 scales=att_scales[:],
                 in_=att_grouped[b][:].rearrange("p m t -> p (m t)"),
             )
+            att_mx[b] = (att_codes, att_scales)
+
+        def second_matmul(b):
+            att_codes, att_scales = att_mx[b]
             v_codes, v_scales = v_mx[b]
-            o_banks[b] = []
             for i in range(D_TILES):
                 o = psum.tile([P, L], F32, tag="o%d" % i)
                 nc.tensor.matmul_mx(
@@ -172,14 +208,14 @@ def tile_dualcrossmodalattention_pa_t_kernel(tc, energy, Wl1, bl1, v2, gamma1, x
                     start=True,
                     stop=True,
                 )
-                o_banks[b].append(o)
+                o_banks[b, i] = o
 
         def gain_and_residual(b):
             result = work.tile([P, D_TILES, L], F32, bufs=3)
             for i in range(D_TILES):
                 nc.vector.scalar_tensor_tensor(
                     out=result[:, i, :],
-                    in0=o_banks[b][i][:],
+                    in0=o_banks[b, i][:],
                     scalar=gamma[:, 0:1],
                     in1=x_rows[b][:, i, :],
                     op0=ALU.mult,
@@ -189,14 +225,21 @@ def tile_dualcrossmodalattention_pa_t_kernel(tc, energy, Wl1, bl1, v2, gamma1, x
                 out=out[b].rearrange("(i p h) j -> p i (h j)", i=D_TILES, h=2), in_=result[:]
             )
 
-        def if_sample(stage, b):
+        def if_sample(stage, b, *half):
             if 0 <= b < B:
-                stage(b)
+                stage(b, *half)
 
-        for s in range(-2, B + 2):
-            if_sample(bias_and_max, s)
-            if_sample(gain_and_residual, s - 2)
-            if_sample(regroup_inputs, s + 2)
-            if_sample(first_matmul, s + 1)
-            if_sample(second_matmul, s - 1)
-            if_sample(softmax, s)
+        for s in range(-4, B + 3):
+            if_sample(add_bias, s + 1, 0)
+            if_sample(softmax_rows, s, 0)
+            if_sample(second_matmul, s - 3)
+            if_sample(first_matmul, s + 1, 1)
+            if_sample(gain_and_residual, s - 3)
+            if_sample(add_bias, s + 1, 1)
+            if_sample(softmax_rows, s, 1)
+            if_sample(regroup_energy, s + 4)
+            if_sample(quantise_att, s - 2)
+            if_sample(quantise_inputs, s + 3)
+            if_sample(first_matmul, s + 2, 0)
+            if_sample(normalise, s)
+            if_sample(regroup_v2, s + 4)

@@ -20,7 +20,7 @@ D_TILES = D // P
 FLOPS = B * (2 * L * L * L + 2 * D * L * L)
 
 
-def k_onto_partitions(nc, psum, identity, rows, grouped):
+def k_onto_partitions(nc, psum, identity, rows, grouped, copy_out):
     row_words = rows.bitcast(F32)
     grouped_words = grouped.bitcast(F32).rearrange("q (c u) -> q c u", u=2)
     for bank in range(2):
@@ -32,7 +32,7 @@ def k_onto_partitions(nc, psum, identity, rows, grouped):
                     row_words[:, 2 * bank + i, u * P : (u + 1) * P],
                     identity,
                 )
-        nc.vector.tensor_copy(
+        copy_out(
             out=grouped_words[:, bank * 2 * P : (bank + 1) * 2 * P, :],
             in_=turned[:].rearrange("q u c -> q c u"),
         )
@@ -51,7 +51,7 @@ def tile_dualcrossmodalattention_pa_t_kernel(tc, energy, Wl1, bl1, v2, gamma1, x
         w_rows = const.tile([P, L_TILES, L], BF16)
         nc.sync.dma_start(out=w_rows[:], in_=Wl1.rearrange("(j p) k -> p j k", p=P))
         bias_rows_bf = const.tile([P, P], BF16)
-        nc.vector.memset(bias_rows_bf[:], 0.0)
+        nc.gpsimd.memset(bias_rows_bf[:], 0.0)
         nc.scalar.dma_start(out=bias_rows_bf[0:L_TILES, :], in_=bl1.rearrange("(j p) -> j p", p=P))
         gamma_bf = const.tile([P, 1], BF16)
         nc.scalar.dma_start(out=gamma_bf[:], in_=gamma1.partition_broadcast(P))
@@ -72,30 +72,30 @@ def tile_dualcrossmodalattention_pa_t_kernel(tc, energy, Wl1, bl1, v2, gamma1, x
         make_identity(nc, identity[:])
 
         w_grouped = const.tile([P, PACK * L], BF16, align_bytes=64)
-        k_onto_partitions(nc, psum, identity[:], w_rows[:], w_grouped[:])
+        k_onto_partitions(nc, psum, identity[:], w_rows[:], w_grouped[:], nc.scalar.copy)
         w_codes = const.tile([P, L], U32, align_bytes=64)
         w_scales = const.tile([P, L], U8, align_bytes=64)
         nc.vector.quantize_mx(out=w_codes[:].bitcast(FP8X4), scales=w_scales[:], in_=w_grouped[:])
 
         bias_rows = const.tile([P, P], F32)
-        nc.vector.tensor_copy(out=bias_rows[:], in_=bias_rows_bf[:])
+        nc.gpsimd.tensor_copy(out=bias_rows[:], in_=bias_rows_bf[:])
         bias_turned = psum.tile([P, P], F32, tag="o0")
         nc.tensor.transpose(bias_turned[:], bias_rows[:], identity[:])
         bias_col = const.tile([P, L_TILES], F32)
-        nc.vector.tensor_copy(out=bias_col[:], in_=bias_turned[:, 0:L_TILES])
+        nc.scalar.copy(out=bias_col[:], in_=bias_turned[:, 0:L_TILES])
         gamma = const.tile([P, 1], F32)
-        nc.vector.tensor_copy(out=gamma[:], in_=gamma_bf[:])
+        nc.gpsimd.tensor_copy(out=gamma[:], in_=gamma_bf[:])
 
         e_grouped, v_grouped, e_mx, v_mx, z_banks, logits = {}, {}, {}, {}, {}, {}
         neg_max, row_sum, exps, att_grouped, att_mx, o_banks = {}, {}, {}, {}, {}, {}
 
         def regroup_energy(b):
             e_group = work.tile([P, PACK * L], BF16, align_bytes=64)
-            k_onto_partitions(nc, psum, identity[:], energy_rows[b][:], e_group[:])
+            k_onto_partitions(nc, psum, identity[:], energy_rows[b][:], e_group[:], nc.vector.tensor_copy)
             e_grouped[b] = e_group
 
         def regroup_v2(b):
-            v_group = work.tile([P, D, PACK], BF16, align_bytes=64)
+            v_group = work.tile([P, D, PACK], BF16, align_bytes=64, bufs=3)
             nc.scalar.copy(
                 out=v_group[:].rearrange("p (c i) t -> p c t i", i=4),
                 in_=v2_rows[b][:].rearrange("p t (c i) -> p c t i", i=4),
@@ -176,7 +176,8 @@ def tile_dualcrossmodalattention_pa_t_kernel(tc, energy, Wl1, bl1, v2, gamma1, x
             inv_sum = work.tile([P, L_TILES], F32, bufs=3)
             nc.vector.reciprocal(out=inv_sum[:], in_=row_sum[b][:])
             att_group = work.tile([P, L, PACK], BF16, align_bytes=64)
-            nc.gpsimd.tensor_tensor(
+            engine = nc.vector if b == B - 1 else nc.gpsimd
+            engine.tensor_tensor(
                 out=att_group[:],
                 in0=exps[b][:].rearrange("p t m -> p m t"),
                 in1=inv_sum[:].unsqueeze(1).to_broadcast([P, L, PACK]),
@@ -212,6 +213,7 @@ def tile_dualcrossmodalattention_pa_t_kernel(tc, energy, Wl1, bl1, v2, gamma1, x
 
         def gain_and_residual(b):
             result = work.tile([P, D_TILES, L], F32, bufs=3)
+            out_rows = out[b].rearrange("(i p h) j -> p i (h j)", i=D_TILES, h=2)
             for i in range(D_TILES):
                 nc.vector.scalar_tensor_tensor(
                     out=result[:, i, :],
@@ -221,9 +223,7 @@ def tile_dualcrossmodalattention_pa_t_kernel(tc, energy, Wl1, bl1, v2, gamma1, x
                     op0=ALU.mult,
                     op1=ALU.add,
                 )
-            nc.sync.dma_start(
-                out=out[b].rearrange("(i p h) j -> p i (h j)", i=D_TILES, h=2), in_=result[:]
-            )
+                nc.sync.dma_start(out=out_rows[:, i, :], in_=result[:, i, :])
 
         def if_sample(stage, b, *half):
             if 0 <= b < B:
@@ -237,9 +237,9 @@ def tile_dualcrossmodalattention_pa_t_kernel(tc, energy, Wl1, bl1, v2, gamma1, x
             if_sample(gain_and_residual, s - 3)
             if_sample(add_bias, s + 1, 1)
             if_sample(softmax_rows, s, 1)
-            if_sample(regroup_energy, s + 4)
             if_sample(quantise_att, s - 2)
             if_sample(quantise_inputs, s + 3)
             if_sample(first_matmul, s + 2, 0)
             if_sample(normalise, s)
+            if_sample(regroup_energy, s + 4)
             if_sample(regroup_v2, s + 4)

@@ -178,9 +178,9 @@ def tile_dualcrossmodalattention_pa_t_kernel(tc, energy, Wl1, bl1, v2, gamma1, x
             att_group = work.tile([P, L, PACK], BF16, align_bytes=64)
             engine = nc.vector if b == B - 1 else nc.gpsimd
             engine.tensor_tensor(
-                out=att_group[:],
-                in0=exps[b][:].rearrange("p t m -> p m t"),
-                in1=inv_sum[:].unsqueeze(1).to_broadcast([P, L, PACK]),
+                out=att_group[:].rearrange("p (c i) t -> p c t i", i=4),
+                in0=exps[b][:].rearrange("p t (c i) -> p c t i", i=4),
+                in1=inv_sum[:].unsqueeze(1).unsqueeze(3).to_broadcast([P, L // 4, PACK, 4]),
                 op=ALU.mult,
             )
             att_grouped[b] = att_group

@@ -17,12 +17,13 @@ PACK = 4
 L_TILES = L // P
 D_TILES = D // P
 
+V_LAG = 2
 FLOPS = B * (2 * L * L * L + 2 * D * L * L)
 
 
-def k_onto_partitions(nc, psum, identity, rows, grouped, copy_out):
+def turn(nc, psum, identity, rows):
     row_words = rows.bitcast(F32)
-    grouped_words = grouped.bitcast(F32).rearrange("q (c u) -> q c u", u=2)
+    banks = []
     for bank in range(2):
         turned = psum.tile([P, 2, 2 * P], F32, tag="turned%d" % bank)
         for i in range(2):
@@ -32,10 +33,16 @@ def k_onto_partitions(nc, psum, identity, rows, grouped, copy_out):
                     row_words[:, 2 * bank + i, u * P : (u + 1) * P],
                     identity,
                 )
-        copy_out(
-            out=grouped_words[:, bank * 2 * P : (bank + 1) * 2 * P, :],
-            in_=turned[:].rearrange("q u c -> q c u"),
-        )
+        banks.append(turned)
+    return banks
+
+
+def empty_bank(turned, grouped, bank, copy_out):
+    grouped_words = grouped.bitcast(F32).rearrange("q (c u) -> q c u", u=2)
+    copy_out(
+        out=grouped_words[:, bank * 2 * P : (bank + 1) * 2 * P, :],
+        in_=turned[bank][:].rearrange("q u c -> q c u"),
+    )
 
 
 def tile_dualcrossmodalattention_pa_t_kernel(tc, energy, Wl1, bl1, v2, gamma1, x, out):
@@ -45,11 +52,9 @@ def tile_dualcrossmodalattention_pa_t_kernel(tc, energy, Wl1, bl1, v2, gamma1, x
         const = ctx.enter_context(tc.tile_pool(name="const", bufs=1))
         inputs = ctx.enter_context(tc.tile_pool(name="inputs", bufs=B))
         work = ctx.enter_context(tc.tile_pool(name="work", bufs=2))
-        held = ctx.enter_context(tc.tile_pool(name="held", bufs=6))
+        held = ctx.enter_context(tc.tile_pool(name="held", bufs=3))
         psum = ctx.enter_context(tc.psum_pool(name="psum", bufs=1))
 
-        w_rows = const.tile([P, L_TILES, L], BF16)
-        nc.sync.dma_start(out=w_rows[:], in_=Wl1.rearrange("(j p) k -> p j k", p=P))
         bias_rows_bf = const.tile([P, P], BF16)
         nc.gpsimd.memset(bias_rows_bf[:], 0.0)
         nc.scalar.dma_start(out=bias_rows_bf[0:L_TILES, :], in_=bl1.rearrange("(j p) -> j p", p=P))
@@ -57,42 +62,39 @@ def tile_dualcrossmodalattention_pa_t_kernel(tc, energy, Wl1, bl1, v2, gamma1, x
         nc.scalar.dma_start(out=gamma_bf[:], in_=gamma1.partition_broadcast(P))
 
         energy_rows, v2_rows, x_rows = [], [], []
-        for b in range(B):
-            e_in = inputs.tile([P, PACK, L], BF16, tag="energy")
-            nc.sync.dma_start(out=e_in[:], in_=energy[b].rearrange("(p t) k -> p t k", t=PACK))
-            energy_rows.append(e_in)
-            v_in = inputs.tile([P, PACK, D], BF16, tag="v2")
-            nc.sync.dma_start(out=v_in[:], in_=v2[b].rearrange("(p t) d -> p t d", t=PACK))
-            v2_rows.append(v_in)
-            x_in = inputs.tile([P, D_TILES, L], BF16, tag="x")
-            nc.sync.dma_start(out=x_in[:], in_=x[b].rearrange("(i p h) j -> p i (h j)", i=D_TILES, h=2))
-            x_rows.append(x_in)
+        for b in range(B + V_LAG):
+            if b < B:
+                e_in = inputs.tile([P, PACK, L], BF16, tag="energy")
+                nc.sync.dma_start(out=e_in[:], in_=energy[b].rearrange("(p t) k -> p t k", t=PACK))
+                energy_rows.append(e_in)
+            if b == 0:
+                w_rows = const.tile([P, L_TILES, L], BF16)
+                nc.sync.dma_start(out=w_rows[:], in_=Wl1.rearrange("(j p) k -> p j k", p=P))
+            if b >= V_LAG:
+                c = b - V_LAG
+                v_in = inputs.tile([P, PACK, D], BF16, tag="v2")
+                nc.sync.dma_start(out=v_in[:], in_=v2[c].rearrange("(p t) d -> p t d", t=PACK))
+                v2_rows.append(v_in)
+                x_in = inputs.tile([P, D_TILES, L], BF16, tag="x")
+                nc.sync.dma_start(out=x_in[:], in_=x[c].rearrange("(i p h) j -> p i (h j)", i=D_TILES, h=2))
+                x_rows.append(x_in)
 
         identity = const.tile([P, P], F32)
         make_identity(nc, identity[:])
 
-        w_grouped = const.tile([P, PACK * L], BF16, align_bytes=64)
-        k_onto_partitions(nc, psum, identity[:], w_rows[:], w_grouped[:], nc.scalar.copy)
-        w_codes = const.tile([P, L], U32, align_bytes=64)
-        w_scales = const.tile([P, L], U8, align_bytes=64)
-        nc.vector.quantize_mx(out=w_codes[:].bitcast(FP8X4), scales=w_scales[:], in_=w_grouped[:])
-
-        bias_rows = const.tile([P, P], F32)
-        nc.gpsimd.tensor_copy(out=bias_rows[:], in_=bias_rows_bf[:])
-        bias_turned = psum.tile([P, P], F32, tag="o0")
-        nc.tensor.transpose(bias_turned[:], bias_rows[:], identity[:])
-        bias_col = const.tile([P, L_TILES], F32)
-        nc.scalar.copy(out=bias_col[:], in_=bias_turned[:, 0:L_TILES])
-        gamma = const.tile([P, 1], F32)
-        nc.gpsimd.tensor_copy(out=gamma[:], in_=gamma_bf[:])
-
         e_grouped, v_grouped, e_mx, v_mx, z_banks, logits = {}, {}, {}, {}, {}, {}
         neg_max, row_sum, exps, att_grouped, att_mx, o_banks = {}, {}, {}, {}, {}, {}
 
-        def regroup_energy(b):
-            e_group = work.tile([P, PACK * L], BF16, align_bytes=64)
-            k_onto_partitions(nc, psum, identity[:], energy_rows[b][:], e_group[:], nc.vector.tensor_copy)
-            e_grouped[b] = e_group
+        turned_banks = {}
+
+        def turn_energy(b):
+            turned_banks[b] = turn(nc, psum, identity[:], energy_rows[b][:])
+
+        def empty_energy(b, bank):
+            if bank == 0:
+                e_group = work.tile([P, PACK * L], BF16, align_bytes=64)
+                e_grouped[b] = e_group
+            empty_bank(turned_banks[b], e_grouped[b][:], bank, nc.vector.tensor_copy)
 
         def regroup_v2(b):
             v_group = work.tile([P, D, PACK], BF16, align_bytes=64, bufs=3)
@@ -102,11 +104,13 @@ def tile_dualcrossmodalattention_pa_t_kernel(tc, energy, Wl1, bl1, v2, gamma1, x
             )
             v_grouped[b] = v_group
 
-        def quantise_inputs(b):
+        def quantise_energy(b):
             e_codes = work.tile([P, L], U32, align_bytes=64, bufs=3)
             e_scales = work.tile([P, L], U8, align_bytes=64, bufs=3)
             nc.vector.quantize_mx(out=e_codes[:].bitcast(FP8X4), scales=e_scales[:], in_=e_grouped[b][:])
             e_mx[b] = (e_codes, e_scales)
+
+        def quantise_v2(b):
             v_codes = held.tile([P, D], U32, align_bytes=64)
             v_scales = held.tile([P, D], U8, align_bytes=64)
             nc.vector.quantize_mx(
@@ -229,17 +233,42 @@ def tile_dualcrossmodalattention_pa_t_kernel(tc, energy, Wl1, bl1, v2, gamma1, x
             if 0 <= b < B:
                 stage(b, *half)
 
-        for s in range(-4, B + 3):
+        turn_energy(0)
+        empty_energy(0, 0)
+        empty_energy(0, 1)
+        w_grouped = const.tile([P, PACK * L], BF16, align_bytes=64)
+        w_turned = turn(nc, psum, identity[:], w_rows[:])
+        for bank in range(2):
+            empty_bank(w_turned, w_grouped[:], bank, nc.scalar.copy)
+        w_codes = const.tile([P, L], U32, align_bytes=64)
+        w_scales = const.tile([P, L], U8, align_bytes=64)
+        nc.vector.quantize_mx(out=w_codes[:].bitcast(FP8X4), scales=w_scales[:], in_=w_grouped[:])
+
+        bias_rows = const.tile([P, P], F32)
+        nc.gpsimd.tensor_copy(out=bias_rows[:], in_=bias_rows_bf[:])
+        bias_turned = psum.tile([P, P], F32, tag="o0")
+        nc.tensor.transpose(bias_turned[:], bias_rows[:], identity[:])
+        bias_col = const.tile([P, L_TILES], F32)
+        nc.scalar.copy(out=bias_col[:], in_=bias_turned[:, 0:L_TILES])
+        gamma = const.tile([P, 1], F32)
+        nc.gpsimd.tensor_copy(out=gamma[:], in_=gamma_bf[:])
+
+        for s in range(-3, B + 2):
             if_sample(add_bias, s + 1, 0)
             if_sample(softmax_rows, s, 0)
-            if_sample(second_matmul, s - 3)
+            if_sample(second_matmul, s - 2)
             if_sample(first_matmul, s + 1, 1)
-            if_sample(gain_and_residual, s - 3)
+            if_sample(gain_and_residual, s - 2)
             if_sample(add_bias, s + 1, 1)
             if_sample(softmax_rows, s, 1)
-            if_sample(quantise_att, s - 2)
-            if_sample(quantise_inputs, s + 3)
+            if s > -3:
+                if_sample(turn_energy, s + 3)
+            if_sample(quantise_energy, s + 2)
+            if_sample(quantise_att, s - 1)
+            if_sample(quantise_v2, s - 1)
             if_sample(first_matmul, s + 2, 0)
             if_sample(normalise, s)
-            if_sample(regroup_energy, s + 4)
-            if_sample(regroup_v2, s + 4)
+            if s > -3:
+                if_sample(empty_energy, s + 3, 0)
+                if_sample(empty_energy, s + 3, 1)
+            if_sample(regroup_v2, s)

@@ -21,27 +21,24 @@ V_LAG = 2
 FLOPS = B * (2 * L * L * L + 2 * D * L * L)
 
 
-def turn(nc, psum, identity, rows):
+def turn_bank(nc, psum, identity, rows, bank, tag):
     row_words = rows.bitcast(F32)
-    banks = []
-    for bank in range(2):
-        turned = psum.tile([P, 2, 2 * P], F32, tag="turned%d" % bank)
-        for i in range(2):
-            for u in range(2):
-                nc.tensor.transpose(
-                    turned[:, u, i * P : (i + 1) * P],
-                    row_words[:, 2 * bank + i, u * P : (u + 1) * P],
-                    identity,
-                )
-        banks.append(turned)
-    return banks
+    turned = psum.tile([P, 2, 2 * P], F32, tag=tag)
+    for i in range(2):
+        for u in range(2):
+            nc.tensor.transpose(
+                turned[:, u, i * P : (i + 1) * P],
+                row_words[:, 2 * bank + i, u * P : (u + 1) * P],
+                identity,
+            )
+    return turned
 
 
 def empty_bank(turned, grouped, bank, copy_out):
     grouped_words = grouped.bitcast(F32).rearrange("q (c u) -> q c u", u=2)
     copy_out(
         out=grouped_words[:, bank * 2 * P : (bank + 1) * 2 * P, :],
-        in_=turned[bank][:].rearrange("q u c -> q c u"),
+        in_=turned[:].rearrange("q u c -> q c u"),
     )
 
 
@@ -87,14 +84,14 @@ def tile_dualcrossmodalattention_pa_t_kernel(tc, energy, Wl1, bl1, v2, gamma1, x
 
         turned_banks = {}
 
-        def turn_energy(b):
-            turned_banks[b] = turn(nc, psum, identity[:], energy_rows[b][:])
+        def turn_energy(b, bank):
+            turned_banks[b, bank] = turn_bank(nc, psum, identity[:], energy_rows[b][:], bank, "turned%d" % bank)
 
-        def empty_energy(b, bank):
+        def empty_energy(b, bank, on_scalar=False):
             if bank == 0:
                 e_group = work.tile([P, PACK * L], BF16, align_bytes=64)
                 e_grouped[b] = e_group
-            empty_bank(turned_banks[b], e_grouped[b][:], bank, nc.vector.tensor_copy)
+            empty_bank(turned_banks[b, bank], e_grouped[b][:], bank, nc.scalar.copy if on_scalar else nc.vector.tensor_copy)
 
         def regroup_v2(b):
             v_group = work.tile([P, D, PACK], BF16, align_bytes=64, bufs=3)
@@ -120,10 +117,10 @@ def tile_dualcrossmodalattention_pa_t_kernel(tc, energy, Wl1, bl1, v2, gamma1, x
             )
             v_mx[b] = (v_codes, v_scales)
 
-        def first_matmul(b, half):
+        def first_matmul(b, *js):
             e_codes, e_scales = e_mx[b]
-            for j in (2 * half, 2 * half + 1):
-                z = psum.tile([P, L], F32, tag="z%d" % (j % 2))
+            for j in js:
+                z = psum.tile([P, L], F32, tag=("z0", "z1", "o0", "o1")[j] if b == 0 else "z%d" % (j % 2))
                 nc.tensor.matmul_mx(
                     out=z[:],
                     lhsT=w_codes[:, j * P : (j + 1) * P].bitcast(FP8X4),
@@ -135,11 +132,15 @@ def tile_dualcrossmodalattention_pa_t_kernel(tc, energy, Wl1, bl1, v2, gamma1, x
                 )
                 z_banks[b, j] = z
 
-        def add_bias(b, half):
-            if half == 0:
+        def add_bias_v(b, *js):
+            for j in js:
+                nc.vector.tensor_scalar(out=logits[b][:, j, :], in0=z_banks[b, j][:], scalar1=bias_col[:, j : j + 1], scalar2=None, op0=ALU.add)
+
+        def add_bias(b, *js):
+            if 0 in js:
                 logit = work.tile([P, L_TILES, L], F32)
                 logits[b] = logit
-            for j in (2 * half, 2 * half + 1):
+            for j in js:
                 nc.scalar.activation(
                     out=logits[b][:, j, :],
                     in_=z_banks[b, j][:],
@@ -148,46 +149,64 @@ def tile_dualcrossmodalattention_pa_t_kernel(tc, energy, Wl1, bl1, v2, gamma1, x
                     scale=1.0,
                 )
 
-        def softmax_rows(b, half):
-            if half == 0:
-                minus_max = work.tile([P, L_TILES], F32, bufs=3)
-                sums = work.tile([P, L_TILES], F32, bufs=3)
-                exp_tile = work.tile([P, L_TILES, L], F32)
-                neg_max[b], row_sum[b], exps[b] = minus_max, sums, exp_tile
-            for t in (2 * half, 2 * half + 1):
+        rows_banks = {}
+
+        def turn_logits(b, *ts):
+            for t in ts:
                 rows = psum.tile([P, L], F32, tag="rows%d" % (t % 2))
                 for j in range(L_TILES):
                     nc.tensor.transpose(
                         rows[:, j * P : (j + 1) * P], logits[b][:, j, t * P : (t + 1) * P], identity[:]
                     )
+                rows_banks[b, t] = rows
+
+        def row_max(b, *ts):
+            if 0 in ts:
+                minus_max = work.tile([P, L_TILES], F32, bufs=3)
+                neg_max[b] = minus_max
+            for t in ts:
                 nc.vector.tensor_reduce(
                     out=neg_max[b][:, t : t + 1],
-                    in_=rows[:],
+                    in_=rows_banks[b, t][:],
                     axis=mybir.AxisListType.X,
                     op=ALU.max,
                     negate=True,
                 )
+
+        def exponentials(b, *ts):
+            if 0 in ts:
+                sums = work.tile([P, L_TILES], F32, bufs=3)
+                exp_tile = work.tile([P, L_TILES, L], F32)
+                row_sum[b], exps[b] = sums, exp_tile
+            for t in ts:
                 nc.scalar.activation(
                     out=exps[b][:, t, :],
-                    in_=rows[:],
+                    in_=rows_banks[b, t][:],
                     func=ACT.Exp,
                     bias=neg_max[b][:, t : t + 1],
                     scale=1.0,
                     accum_out=row_sum[b][:, t : t + 1],
                 )
 
-        def normalise(b):
+        inv_sums = {}
+
+        def recip(b):
             inv_sum = work.tile([P, L_TILES], F32, bufs=3)
             nc.vector.reciprocal(out=inv_sum[:], in_=row_sum[b][:])
+            inv_sums[b] = inv_sum
             att_group = work.tile([P, L, PACK], BF16, align_bytes=64)
-            engine = nc.vector if b == B - 1 else nc.gpsimd
+            att_grouped[b] = att_group
+
+        def norm_part(engine, inv, b, lo, hi):
             engine.tensor_tensor(
-                out=att_group[:].rearrange("p (c i) t -> p c t i", i=4),
-                in0=exps[b][:].rearrange("p t (c i) -> p c t i", i=4),
-                in1=inv_sum[:].unsqueeze(1).unsqueeze(3).to_broadcast([P, L // 4, PACK, 4]),
+                out=att_grouped[b][:, lo:hi, :].rearrange("p (c i) t -> p c t i", i=4),
+                in0=exps[b][:, :, lo:hi].rearrange("p t (c i) -> p c t i", i=4),
+                in1=inv[:].unsqueeze(1).unsqueeze(3).to_broadcast([P, (hi - lo) // 4, PACK, 4]),
                 op=ALU.mult,
             )
-            att_grouped[b] = att_group
+
+        def normalise(b):
+            norm_part(nc.vector if b == B - 1 else nc.gpsimd, inv_sums[b], b, 0, L)
 
         def quantise_att(b):
             att_codes = work.tile([P, L], U32, align_bytes=64)
@@ -199,10 +218,10 @@ def tile_dualcrossmodalattention_pa_t_kernel(tc, energy, Wl1, bl1, v2, gamma1, x
             )
             att_mx[b] = (att_codes, att_scales)
 
-        def second_matmul(b):
+        def second_matmul(b, *tiles):
             att_codes, att_scales = att_mx[b]
             v_codes, v_scales = v_mx[b]
-            for i in range(D_TILES):
+            for i in tiles:
                 o = psum.tile([P, L], F32, tag="o%d" % i)
                 nc.tensor.matmul_mx(
                     out=o[:],
@@ -215,10 +234,15 @@ def tile_dualcrossmodalattention_pa_t_kernel(tc, energy, Wl1, bl1, v2, gamma1, x
                 )
                 o_banks[b, i] = o
 
-        def gain_and_residual(b):
-            result = work.tile([P, D_TILES, L], F32, bufs=3)
+        results = {}
+
+        def gain_and_residual(b, *tiles):
+            if 0 in tiles:
+                result = work.tile([P, D_TILES, L], F32, bufs=3)
+                results[b] = result
+            result = results[b]
             out_rows = out[b].rearrange("(i p h) j -> p i (h j)", i=D_TILES, h=2)
-            for i in range(D_TILES):
+            for i in tiles:
                 nc.vector.scalar_tensor_tensor(
                     out=result[:, i, :],
                     in0=o_banks[b, i][:],
@@ -229,46 +253,69 @@ def tile_dualcrossmodalattention_pa_t_kernel(tc, energy, Wl1, bl1, v2, gamma1, x
                 )
                 nc.sync.dma_start(out=out_rows[:, i, :], in_=result[:, i, :])
 
-        def if_sample(stage, b, *half):
+        def do(stage, b, *args):
             if 0 <= b < B:
-                stage(b, *half)
+                stage(b, *args)
 
-        turn_energy(0)
-        empty_energy(0, 0)
+        bias_rows = const.tile([P, P], F32)
+        nc.scalar.copy(out=bias_rows[:], in_=bias_rows_bf[:])
+        turn_energy(0, 0)
+        turn_energy(0, 1)
+        empty_energy(0, 0, True)
         empty_energy(0, 1)
         w_grouped = const.tile([P, PACK * L], BF16, align_bytes=64)
-        w_turned = turn(nc, psum, identity[:], w_rows[:])
-        for bank in range(2):
-            empty_bank(w_turned, w_grouped[:], bank, nc.scalar.copy)
+        w0 = turn_bank(nc, psum, identity[:], w_rows[:], 0, "rows0")
+        w1 = turn_bank(nc, psum, identity[:], w_rows[:], 1, "rows1")
+        bias_turned = psum.tile([P, P], F32, tag="o0")
+        nc.tensor.transpose(bias_turned[:], bias_rows[:], identity[:])
+        turn_energy(1, 0)
+        turn_energy(1, 1)
+        empty_bank(w0, w_grouped[:], 0, nc.scalar.copy)
+        empty_bank(w1, w_grouped[:], 1, nc.vector.tensor_copy)
+        quantise_energy(0)
+        bias_col = const.tile([P, L_TILES], F32)
+        nc.scalar.copy(out=bias_col[:], in_=bias_turned[:, 0:L_TILES])
         w_codes = const.tile([P, L], U32, align_bytes=64)
         w_scales = const.tile([P, L], U8, align_bytes=64)
         nc.vector.quantize_mx(out=w_codes[:].bitcast(FP8X4), scales=w_scales[:], in_=w_grouped[:])
-
-        bias_rows = const.tile([P, P], F32)
-        nc.gpsimd.tensor_copy(out=bias_rows[:], in_=bias_rows_bf[:])
-        bias_turned = psum.tile([P, P], F32, tag="o0")
-        nc.tensor.transpose(bias_turned[:], bias_rows[:], identity[:])
-        bias_col = const.tile([P, L_TILES], F32)
-        nc.scalar.copy(out=bias_col[:], in_=bias_turned[:, 0:L_TILES])
         gamma = const.tile([P, 1], F32)
-        nc.gpsimd.tensor_copy(out=gamma[:], in_=gamma_bf[:])
-
-        for s in range(-3, B + 2):
-            if_sample(add_bias, s + 1, 0)
-            if_sample(softmax_rows, s, 0)
-            if_sample(second_matmul, s - 2)
-            if_sample(first_matmul, s + 1, 1)
-            if_sample(gain_and_residual, s - 2)
-            if_sample(add_bias, s + 1, 1)
-            if_sample(softmax_rows, s, 1)
-            if s > -3:
-                if_sample(turn_energy, s + 3)
-            if_sample(quantise_energy, s + 2)
-            if_sample(quantise_att, s - 1)
-            if_sample(quantise_v2, s - 1)
-            if_sample(first_matmul, s + 2, 0)
-            if_sample(normalise, s)
-            if s > -3:
-                if_sample(empty_energy, s + 3, 0)
-                if_sample(empty_energy, s + 3, 1)
-            if_sample(regroup_v2, s)
+        nc.scalar.copy(out=gamma[:], in_=gamma_bf[:])
+        first_matmul(0, 0, 1, 2, 3)
+        empty_energy(1, 0)
+        empty_energy(1, 1)
+        add_bias(0, 0, 2)
+        add_bias_v(0, 1, 3)
+        quantise_energy(1)
+        turn_logits(0, 0, 1)
+        turn_energy(2, 0)
+        turn_energy(2, 1)
+        first_matmul(1, 0, 1)
+        regroup_v2(0)
+        row_max(0, 0, 1)
+        exponentials(0, 0, 1)
+        empty_energy(2, 0)
+        empty_energy(2, 1)
+        for s in range(B + 2):
+            do(add_bias, s + 1, 0, 1)
+            if s > 0:
+                do(turn_logits, s, 0, 1)
+                do(row_max, s, 0, 1)
+                do(exponentials, s, 0, 1)
+            do(second_matmul, s - 2, 0, 1)
+            do(first_matmul, s + 1, 2, 3)
+            do(gain_and_residual, s - 2, 0, 1)
+            do(add_bias, s + 1, 2, 3)
+            do(turn_logits, s, 2, 3)
+            do(row_max, s, 2, 3)
+            do(exponentials, s, 2, 3)
+            do(turn_energy, s + 3, 0)
+            do(turn_energy, s + 3, 1)
+            do(quantise_energy, s + 2)
+            do(quantise_att, s - 1)
+            do(recip, s)
+            do(quantise_v2, s - 1)
+            do(first_matmul, s + 2, 0, 1)
+            do(normalise, s)
+            do(empty_energy, s + 3, 0)
+            do(empty_energy, s + 3, 1)
+            do(regroup_v2, s + 1)

@@ -17,6 +17,7 @@ PACK = 4
 L_TILES = L // P
 D_TILES = D // P
 
+V_COLUMNS = 128
 V_LAG = 2
 FLOPS = B * (2 * L * L * L + 2 * D * L * L)
 
@@ -34,11 +35,11 @@ def turn_bank(nc, psum, identity, rows, bank, tag):
     return turned
 
 
-def empty_bank(turned, grouped, bank, copy_out):
+def empty_bank(turned, grouped, bank, copy_out, lo=0, hi=2 * P):
     grouped_words = grouped.bitcast(F32).rearrange("q (c u) -> q c u", u=2)
     copy_out(
-        out=grouped_words[:, bank * 2 * P : (bank + 1) * 2 * P, :],
-        in_=turned[:].rearrange("q u c -> q c u"),
+        out=grouped_words[:, bank * 2 * P + lo : bank * 2 * P + hi, :],
+        in_=turned[:, :, lo:hi].rearrange("q u c -> q c u"),
     )
 
 
@@ -49,7 +50,7 @@ def tile_dualcrossmodalattention_pa_t_kernel(tc, energy, Wl1, bl1, v2, gamma1, x
         const = ctx.enter_context(tc.tile_pool(name="const", bufs=1))
         inputs = ctx.enter_context(tc.tile_pool(name="inputs", bufs=B))
         work = ctx.enter_context(tc.tile_pool(name="work", bufs=2))
-        held = ctx.enter_context(tc.tile_pool(name="held", bufs=3))
+        held = ctx.enter_context(tc.tile_pool(name="held", bufs=4))
         psum = ctx.enter_context(tc.psum_pool(name="psum", bufs=1))
 
         bias_rows_bf = const.tile([P, P], BF16)
@@ -91,7 +92,13 @@ def tile_dualcrossmodalattention_pa_t_kernel(tc, energy, Wl1, bl1, v2, gamma1, x
             if bank == 0:
                 e_group = work.tile([P, PACK * L], BF16, align_bytes=64)
                 e_grouped[b] = e_group
-            empty_bank(turned_banks[b, bank], e_grouped[b][:], bank, nc.scalar.copy if on_scalar else nc.vector.tensor_copy)
+            if on_scalar:
+                empty_bank(turned_banks[b, bank], e_grouped[b][:], bank, nc.scalar.copy)
+            elif bank == 1:
+                empty_bank(turned_banks[b, bank], e_grouped[b][:], bank, nc.vector.tensor_copy)
+            else:
+                empty_bank(turned_banks[b, bank], e_grouped[b][:], bank, nc.scalar.copy, V_COLUMNS, 2 * P)
+                empty_bank(turned_banks[b, bank], e_grouped[b][:], bank, nc.vector.tensor_copy, 0, V_COLUMNS)
 
         def regroup_v2(b):
             v_group = work.tile([P, D, PACK], BF16, align_bytes=64, bufs=3)
@@ -295,7 +302,7 @@ def tile_dualcrossmodalattention_pa_t_kernel(tc, energy, Wl1, bl1, v2, gamma1, x
         exponentials(0, 0, 1)
         empty_energy(2, 0)
         empty_energy(2, 1)
-        for s in range(B + 2):
+        for s in range(B):
             do(add_bias, s + 1, 0, 1)
             if s > 0:
                 do(turn_logits, s, 0, 1)
@@ -313,9 +320,16 @@ def tile_dualcrossmodalattention_pa_t_kernel(tc, energy, Wl1, bl1, v2, gamma1, x
             do(quantise_energy, s + 2)
             do(quantise_att, s - 1)
             do(recip, s)
-            do(quantise_v2, s - 1)
+            do(quantise_v2, s)
             do(first_matmul, s + 2, 0, 1)
             do(normalise, s)
             do(empty_energy, s + 3, 0)
             do(empty_energy, s + 3, 1)
             do(regroup_v2, s + 1)
+        second_matmul(B - 2, 0, 1)
+        gain_and_residual(B - 2, 0)
+        quantise_att(B - 1)
+        second_matmul(B - 1, 0)
+        gain_and_residual(B - 2, 1)
+        second_matmul(B - 1, 1)
+        gain_and_residual(B - 1, 0, 1)

@@ -183,12 +183,12 @@ def tile_dualcrossmodalattention_pa_t_kernel(tc, energy, Wl1, bl1, v2, gamma1, x
         def exponentials(b, *ts):
             if 0 in ts:
                 sums = work.tile([P, L_TILES], F32, bufs=3)
-                exp_tile = work.tile([P, L_TILES, L], F32)
+                exp_tile = work.tile([P, L // 4, PACK, 4], F32)
                 row_sum[b], exps[b] = sums, exp_tile
             for t in ts:
                 nc.scalar.activation(
-                    out=exps[b][:, t, :],
-                    in_=rows_banks[b, t][:],
+                    out=exps[b][:, :, t, :],
+                    in_=rows_banks[b, t][:].rearrange("p (c i) -> p c i", i=4),
                     func=ACT.Exp,
                     bias=neg_max[b][:, t : t + 1],
                     scale=1.0,
@@ -207,7 +207,7 @@ def tile_dualcrossmodalattention_pa_t_kernel(tc, energy, Wl1, bl1, v2, gamma1, x
         def norm_part(engine, inv, b, lo, hi):
             engine.tensor_tensor(
                 out=att_grouped[b][:, lo:hi, :].rearrange("p (c i) t -> p c t i", i=4),
-                in0=exps[b][:, :, lo:hi].rearrange("p t (c i) -> p c t i", i=4),
+                in0=exps[b][:, lo // 4 : hi // 4, :, :],
                 in1=inv[:].unsqueeze(1).unsqueeze(3).to_broadcast([P, (hi - lo) // 4, PACK, 4]),
                 op=ALU.mult,
             )

@@ -18,6 +18,8 @@ L_TILES = L // P
 D_TILES = D // P
 
 V_COLUMNS = 128
+HALVES = (slice(0, 2), slice(2, 4))
+G_COLUMNS = 480
 V_LAG = 2
 FLOPS = B * (2 * L * L * L + 2 * D * L * L)
 
@@ -63,11 +65,18 @@ def tile_dualcrossmodalattention_pa_t_kernel(tc, energy, Wl1, bl1, v2, gamma1, x
         for b in range(B + V_LAG):
             if b < B:
                 e_in = inputs.tile([P, PACK, L], BF16, tag="energy")
-                nc.sync.dma_start(out=e_in[:], in_=energy[b].rearrange("(p t) k -> p t k", t=PACK))
+                e_src = energy[b].rearrange("(p t) k -> p t k", t=PACK)
+                if b == 0:
+                    for half in HALVES:
+                        nc.sync.dma_start(out=e_in[:, half, :], in_=e_src[:, half, :])
+                else:
+                    nc.sync.dma_start(out=e_in[:], in_=e_src)
                 energy_rows.append(e_in)
             if b == 0:
                 w_rows = const.tile([P, L_TILES, L], BF16)
-                nc.sync.dma_start(out=w_rows[:], in_=Wl1.rearrange("(j p) k -> p j k", p=P))
+                w_src = Wl1.rearrange("(j p) k -> p j k", p=P)
+                for half in HALVES:
+                    nc.sync.dma_start(out=w_rows[:, half, :], in_=w_src[:, half, :])
             if b >= V_LAG:
                 c = b - V_LAG
                 v_in = inputs.tile([P, PACK, D], BF16, tag="v2")
@@ -138,6 +147,20 @@ def tile_dualcrossmodalattention_pa_t_kernel(tc, energy, Wl1, bl1, v2, gamma1, x
                     stop=True,
                 )
                 z_banks[b, j] = z
+
+        def keep_warm(b, tag):
+            e_codes, e_scales = e_mx[b]
+            for i in range(2):
+                unread = psum.tile([P, L], F32, tag=tag % i)
+                nc.tensor.matmul_mx(
+                    out=unread[:],
+                    lhsT=w_codes[:, 0:P].bitcast(FP8X4),
+                    lhsT_scale=w_scales[:, 0:P],
+                    rhs=e_codes[:].bitcast(FP8X4),
+                    rhs_scale=e_scales[:],
+                    start=True,
+                    stop=True,
+                )
 
         def add_bias_v(b, *js):
             for j in js:
@@ -212,8 +235,11 @@ def tile_dualcrossmodalattention_pa_t_kernel(tc, energy, Wl1, bl1, v2, gamma1, x
                 op=ALU.mult,
             )
 
-        def normalise(b):
-            norm_part(nc.vector if b == B - 1 else nc.gpsimd, inv_sums[b], b, 0, L)
+        def normalise_first(b):
+            norm_part(nc.vector if b == B - 1 else nc.gpsimd, inv_sums[b], b, 0, G_COLUMNS)
+
+        def normalise_rest(b):
+            norm_part(nc.vector, inv_sums[b], b, G_COLUMNS, L)
 
         def quantise_att(b):
             att_codes = work.tile([P, L], U32, align_bytes=64)
@@ -315,19 +341,23 @@ def tile_dualcrossmodalattention_pa_t_kernel(tc, energy, Wl1, bl1, v2, gamma1, x
             do(turn_logits, s, 2, 3)
             do(row_max, s, 2, 3)
             do(exponentials, s, 2, 3)
+            do(keep_warm, s + 1, "turned%d")
             do(turn_energy, s + 3, 0)
             do(turn_energy, s + 3, 1)
+            do(keep_warm, s + 1, "z%d")
+            do(normalise_rest, s - 1)
             do(quantise_energy, s + 2)
             do(quantise_att, s - 1)
             do(recip, s)
             do(quantise_v2, s)
             do(first_matmul, s + 2, 0, 1)
-            do(normalise, s)
+            do(normalise_first, s)
             do(empty_energy, s + 3, 0)
             do(empty_energy, s + 3, 1)
             do(regroup_v2, s + 1)
         second_matmul(B - 2, 0, 1)
         gain_and_residual(B - 2, 0)
+        normalise_rest(B - 1)
         quantise_att(B - 1)
         second_matmul(B - 1, 0)
         gain_and_residual(B - 2, 1)

@@ -20,6 +20,7 @@ D_TILES = D // P
 V_COLUMNS = 128
 HALVES = (slice(0, 2), slice(2, 4))
 G_COLUMNS = 480
+LATE_COLUMNS = 384
 V_LAG = 2
 FLOPS = B * (2 * L * L * L + 2 * D * L * L)
 
@@ -236,10 +237,21 @@ def tile_dualcrossmodalattention_pa_t_kernel(tc, energy, Wl1, bl1, v2, gamma1, x
             )
 
         def normalise_first(b):
-            norm_part(nc.vector if b == B - 1 else nc.gpsimd, inv_sums[b], b, 0, G_COLUMNS)
+            norm_part(nc.gpsimd, inv_sums[b], b, 0, G_COLUMNS if b < B - 2 else LATE_COLUMNS)
 
         def normalise_rest(b):
-            norm_part(nc.vector, inv_sums[b], b, G_COLUMNS, L)
+            norm_part(nc.vector, inv_sums[b], b, G_COLUMNS if b < B - 2 else LATE_COLUMNS, L)
+
+        def normalise_last():
+            b = B - 1
+            for t in range(PACK):
+                nc.scalar.activation(
+                    out=att_grouped[b][:, LATE_COLUMNS:, t].rearrange("p (c i) -> p c i", i=4),
+                    in_=exps[b][:, LATE_COLUMNS // 4 :, t, :],
+                    func=ACT.Copy,
+                    scale=inv_sums[b][:, t : t + 1],
+                )
+            norm_part(nc.vector, inv_sums[b], b, 0, LATE_COLUMNS)
 
         def quantise_att(b):
             att_codes = work.tile([P, L], U32, align_bytes=64)
@@ -290,10 +302,20 @@ def tile_dualcrossmodalattention_pa_t_kernel(tc, energy, Wl1, bl1, v2, gamma1, x
             if 0 <= b < B:
                 stage(b, *args)
 
+        zeros = const.tile([P, L], BF16)
+        nc.vector.memset(zeros[:], 0.0)
+
+        def wake(n):
+            for i in range(n):
+                unread = psum.tile([P, L], F32, tag="o1")
+                nc.tensor.matmul(out=unread[:], lhsT=zeros[:, 0:P], rhs=zeros[:], start=True, stop=True)
+
         bias_rows = const.tile([P, P], F32)
         nc.scalar.copy(out=bias_rows[:], in_=bias_rows_bf[:])
+        wake(4)
         turn_energy(0, 0)
         turn_energy(0, 1)
+        wake(2)
         empty_energy(0, 0, True)
         empty_energy(0, 1)
         w_grouped = const.tile([P, PACK * L], BF16, align_bytes=64)
@@ -301,8 +323,10 @@ def tile_dualcrossmodalattention_pa_t_kernel(tc, energy, Wl1, bl1, v2, gamma1, x
         w1 = turn_bank(nc, psum, identity[:], w_rows[:], 1, "rows1")
         bias_turned = psum.tile([P, P], F32, tag="o0")
         nc.tensor.transpose(bias_turned[:], bias_rows[:], identity[:])
+        wake(2)
         turn_energy(1, 0)
         turn_energy(1, 1)
+        wake(3)
         empty_bank(w0, w_grouped[:], 0, nc.scalar.copy)
         empty_bank(w1, w_grouped[:], 1, nc.vector.tensor_copy)
         quantise_energy(0)
@@ -341,23 +365,22 @@ def tile_dualcrossmodalattention_pa_t_kernel(tc, energy, Wl1, bl1, v2, gamma1, x
             do(turn_logits, s, 2, 3)
             do(row_max, s, 2, 3)
             do(exponentials, s, 2, 3)
-            do(keep_warm, s + 1, "turned%d")
+            do(keep_warm, min(s + 1, B - 1), "turned%d")
             do(turn_energy, s + 3, 0)
             do(turn_energy, s + 3, 1)
-            do(keep_warm, s + 1, "z%d")
+            do(keep_warm, min(s + 1, B - 1), "z%d")
             do(normalise_rest, s - 1)
             do(quantise_energy, s + 2)
             do(quantise_att, s - 1)
             do(recip, s)
             do(quantise_v2, s)
             do(first_matmul, s + 2, 0, 1)
-            do(normalise_first, s)
+            do(normalise_first, s) if s < B - 1 else normalise_last()
             do(empty_energy, s + 3, 0)
             do(empty_energy, s + 3, 1)
             do(regroup_v2, s + 1)
         second_matmul(B - 2, 0, 1)
         gain_and_residual(B - 2, 0)
-        normalise_rest(B - 1)
         quantise_att(B - 1)
         second_matmul(B - 1, 0)
         gain_and_residual(B - 2, 1)

@@ -21,6 +21,7 @@ V_COLUMNS = 128
 HALVES = (slice(0, 2), slice(2, 4))
 G_COLUMNS = 480
 LATE_COLUMNS = 384
+RUN = 8
 V_LAG = 2
 FLOPS = B * (2 * L * L * L + 2 * D * L * L)
 
@@ -207,12 +208,12 @@ def tile_dualcrossmodalattention_pa_t_kernel(tc, energy, Wl1, bl1, v2, gamma1, x
         def exponentials(b, *ts):
             if 0 in ts:
                 sums = work.tile([P, L_TILES], F32, bufs=3)
-                exp_tile = work.tile([P, L // 4, PACK, 4], F32)
+                exp_tile = work.tile([P, L // RUN, PACK, RUN], F32)
                 row_sum[b], exps[b] = sums, exp_tile
             for t in ts:
                 nc.scalar.activation(
                     out=exps[b][:, :, t, :],
-                    in_=rows_banks[b, t][:].rearrange("p (c i) -> p c i", i=4),
+                    in_=rows_banks[b, t][:].rearrange("p (c i) -> p c i", i=RUN),
                     func=ACT.Exp,
                     bias=neg_max[b][:, t : t + 1],
                     scale=1.0,
@@ -230,9 +231,9 @@ def tile_dualcrossmodalattention_pa_t_kernel(tc, energy, Wl1, bl1, v2, gamma1, x
 
         def norm_part(engine, inv, b, lo, hi):
             engine.tensor_tensor(
-                out=att_grouped[b][:, lo:hi, :].rearrange("p (c i) t -> p c t i", i=4),
-                in0=exps[b][:, lo // 4 : hi // 4, :, :],
-                in1=inv[:].unsqueeze(1).unsqueeze(3).to_broadcast([P, (hi - lo) // 4, PACK, 4]),
+                out=att_grouped[b][:, lo:hi, :].rearrange("p (c i) t -> p c t i", i=RUN),
+                in0=exps[b][:, lo // RUN : hi // RUN, :, :],
+                in1=inv[:].unsqueeze(1).unsqueeze(3).to_broadcast([P, (hi - lo) // RUN, PACK, RUN]),
                 op=ALU.mult,
             )
 
@@ -246,8 +247,8 @@ def tile_dualcrossmodalattention_pa_t_kernel(tc, energy, Wl1, bl1, v2, gamma1, x
             b = B - 1
             for t in range(PACK):
                 nc.scalar.activation(
-                    out=att_grouped[b][:, LATE_COLUMNS:, t].rearrange("p (c i) -> p c i", i=4),
-                    in_=exps[b][:, LATE_COLUMNS // 4 :, t, :],
+                    out=att_grouped[b][:, LATE_COLUMNS:, t].rearrange("p (c i) -> p c i", i=RUN),
+                    in_=exps[b][:, LATE_COLUMNS // RUN :, t, :],
                     func=ACT.Copy,
                     scale=inv_sums[b][:, t : t + 1],
                 )

@@ -114,8 +114,8 @@ def tile_dualcrossmodalattention_pa_t_kernel(tc, energy, Wl1, bl1, v2, gamma1, x
         def regroup_v2(b):
             v_group = work.tile([P, D, PACK], BF16, align_bytes=64, bufs=3)
             nc.scalar.copy(
-                out=v_group[:].rearrange("p (c i) t -> p c t i", i=4),
-                in_=v2_rows[b][:].rearrange("p t (c i) -> p c t i", i=4),
+                out=v_group[:].rearrange("p (c i) t -> p c t i", i=RUN),
+                in_=v2_rows[b][:].rearrange("p t (c i) -> p c t i", i=RUN),
             )
             v_grouped[b] = v_group
 

from contextlib import ExitStack

from concourse import mybir
from concourse.masks import make_identity

F32 = mybir.dt.float32
BF16 = mybir.dt.bfloat16
U32 = mybir.dt.uint32
U8 = mybir.dt.uint8
FP8X4 = mybir.dt.float8_e4m3fn_x4
ALU = mybir.AluOpType
ACT = mybir.ActivationFunctionType

B, L, D = 16, 512, 256
P = 128
PACK = 4
L_TILES = L // P
D_TILES = D // P

V_COLUMNS = 128
HALVES = (slice(0, 2), slice(2, 4))
G_COLUMNS = 480
LATE_COLUMNS = 384
RUN = 8
V_LAG = 2
FLOPS = B * (2 * L * L * L + 2 * D * L * L)


def turn_bank(nc, psum, identity, rows, bank, tag):
    row_words = rows.bitcast(F32)
    turned = psum.tile([P, 2, 2 * P], F32, tag=tag)
    for i in range(2):
        for u in range(2):
            nc.tensor.transpose(
                turned[:, u, i * P : (i + 1) * P],
                row_words[:, 2 * bank + i, u * P : (u + 1) * P],
                identity,
            )
    return turned


def empty_bank(turned, grouped, bank, copy_out, lo=0, hi=2 * P):
    grouped_words = grouped.bitcast(F32).rearrange("q (c u) -> q c u", u=2)
    copy_out(
        out=grouped_words[:, bank * 2 * P + lo : bank * 2 * P + hi, :],
        in_=turned[:, :, lo:hi].rearrange("q u c -> q c u"),
    )


def tile_dualcrossmodalattention_pa_t_kernel(tc, energy, Wl1, bl1, v2, gamma1, x, out):
    nc = tc.nc
    with ExitStack() as ctx:
        ctx.enter_context(tc.manual_schedule())
        const = ctx.enter_context(tc.tile_pool(name="const", bufs=1))
        inputs = ctx.enter_context(tc.tile_pool(name="inputs", bufs=B))
        work = ctx.enter_context(tc.tile_pool(name="work", bufs=2))
        held = ctx.enter_context(tc.tile_pool(name="held", bufs=4))
        psum = ctx.enter_context(tc.psum_pool(name="psum", bufs=1))

        bias_rows_bf = const.tile([P, P], BF16)
        nc.gpsimd.memset(bias_rows_bf[:], 0.0)
        nc.scalar.dma_start(out=bias_rows_bf[0:L_TILES, :], in_=bl1.rearrange("(j p) -> j p", p=P))
        gamma_bf = const.tile([P, 1], BF16)
        nc.scalar.dma_start(out=gamma_bf[:], in_=gamma1.partition_broadcast(P))

        energy_rows, v2_rows, x_rows = [], [], []
        for b in range(B + V_LAG):
            if b < B:
                e_in = inputs.tile([P, PACK, L], BF16, tag="energy")
                e_src = energy[b].rearrange("(p t) k -> p t k", t=PACK)
                if b == 0:
                    for half in HALVES:
                        nc.sync.dma_start(out=e_in[:, half, :], in_=e_src[:, half, :])
                else:
                    nc.sync.dma_start(out=e_in[:], in_=e_src)
                energy_rows.append(e_in)
            if b == 0:
                w_rows = const.tile([P, L_TILES, L], BF16)
                w_src = Wl1.rearrange("(j p) k -> p j k", p=P)
                for half in HALVES:
                    nc.sync.dma_start(out=w_rows[:, half, :], in_=w_src[:, half, :])
            if b >= V_LAG:
                c = b - V_LAG
                v_in = inputs.tile([P, PACK, D], BF16, tag="v2")
                nc.sync.dma_start(out=v_in[:], in_=v2[c].rearrange("(p t) d -> p t d", t=PACK))
                v2_rows.append(v_in)
                x_in = inputs.tile([P, D_TILES, L], BF16, tag="x")
                nc.sync.dma_start(out=x_in[:], in_=x[c].rearrange("(i p h) j -> p i (h j)", i=D_TILES, h=2))
                x_rows.append(x_in)

        identity = const.tile([P, P], F32)
        make_identity(nc, identity[:])

        e_grouped, v_grouped, e_mx, v_mx, z_banks, logits = {}, {}, {}, {}, {}, {}
        neg_max, row_sum, exps, att_grouped, att_mx, o_banks = {}, {}, {}, {}, {}, {}

        turned_banks = {}

        def turn_energy(b, bank):
            turned_banks[b, bank] = turn_bank(nc, psum, identity[:], energy_rows[b][:], bank, "turned%d" % bank)

        def empty_energy(b, bank, on_scalar=False):
            if bank == 0:
                e_group = work.tile([P, PACK * L], BF16, align_bytes=64)
                e_grouped[b] = e_group
            if on_scalar:
                empty_bank(turned_banks[b, bank], e_grouped[b][:], bank, nc.scalar.copy)
            elif bank == 1:
                empty_bank(turned_banks[b, bank], e_grouped[b][:], bank, nc.vector.tensor_copy)
            else:
                empty_bank(turned_banks[b, bank], e_grouped[b][:], bank, nc.scalar.copy, V_COLUMNS, 2 * P)
                empty_bank(turned_banks[b, bank], e_grouped[b][:], bank, nc.vector.tensor_copy, 0, V_COLUMNS)

        def regroup_v2(b):
            v_group = work.tile([P, D, PACK], BF16, align_bytes=64, bufs=3)
            nc.scalar.copy(
                out=v_group[:].rearrange("p (c i) t -> p c t i", i=RUN),
                in_=v2_rows[b][:].rearrange("p t (c i) -> p c t i", i=RUN),
            )
            v_grouped[b] = v_group

        def quantise_energy(b):
            e_codes = work.tile([P, L], U32, align_bytes=64, bufs=3)
            e_scales = work.tile([P, L], U8, align_bytes=64, bufs=3)
            nc.vector.quantize_mx(out=e_codes[:].bitcast(FP8X4), scales=e_scales[:], in_=e_grouped[b][:])
            e_mx[b] = (e_codes, e_scales)

        def quantise_v2(b):
            v_codes = held.tile([P, D], U32, align_bytes=64)
            v_scales = held.tile([P, D], U8, align_bytes=64)
            nc.vector.quantize_mx(
                out=v_codes[:].bitcast(FP8X4),
                scales=v_scales[:],
                in_=v_grouped[b][:].rearrange("p d t -> p (d t)"),
            )
            v_mx[b] = (v_codes, v_scales)

        def first_matmul(b, *js):
            e_codes, e_scales = e_mx[b]
            for j in js:
                z = psum.tile([P, L], F32, tag=("z0", "z1", "o0", "o1")[j] if b == 0 else "z%d" % (j % 2))
                nc.tensor.matmul_mx(
                    out=z[:],
                    lhsT=w_codes[:, j * P : (j + 1) * P].bitcast(FP8X4),
                    lhsT_scale=w_scales[:, j * P : (j + 1) * P],
                    rhs=e_codes[:].bitcast(FP8X4),
                    rhs_scale=e_scales[:],
                    start=True,
                    stop=True,
                )
                z_banks[b, j] = z

        def keep_warm(b, tag):
            e_codes, e_scales = e_mx[b]
            for i in range(2):
                unread = psum.tile([P, L], F32, tag=tag % i)
                nc.tensor.matmul_mx(
                    out=unread[:],
                    lhsT=w_codes[:, 0:P].bitcast(FP8X4),
                    lhsT_scale=w_scales[:, 0:P],
                    rhs=e_codes[:].bitcast(FP8X4),
                    rhs_scale=e_scales[:],
                    start=True,
                    stop=True,
                )

        def add_bias_v(b, *js):
            for j in js:
                nc.vector.tensor_scalar(out=logits[b][:, j, :], in0=z_banks[b, j][:], scalar1=bias_col[:, j : j + 1], scalar2=None, op0=ALU.add)

        def add_bias(b, *js):
            if 0 in js:
                logit = work.tile([P, L_TILES, L], F32)
                logits[b] = logit
            for j in js:
                nc.scalar.activation(
                    out=logits[b][:, j, :],
                    in_=z_banks[b, j][:],
                    func=ACT.Identity,
                    bias=bias_col[:, j : j + 1],
                    scale=1.0,
                )

        rows_banks = {}

        def turn_logits(b, *ts):
            for t in ts:
                rows = psum.tile([P, L], F32, tag="rows%d" % (t % 2))
                for j in range(L_TILES):
                    nc.tensor.transpose(
                        rows[:, j * P : (j + 1) * P], logits[b][:, j, t * P : (t + 1) * P], identity[:]
                    )
                rows_banks[b, t] = rows

        def row_max(b, *ts):
            if 0 in ts:
                minus_max = work.tile([P, L_TILES], F32, bufs=3)
                neg_max[b] = minus_max
            for t in ts:
                nc.vector.tensor_reduce(
                    out=neg_max[b][:, t : t + 1],
                    in_=rows_banks[b, t][:],
                    axis=mybir.AxisListType.X,
                    op=ALU.max,
                    negate=True,
                )

        def exponentials(b, *ts):
            if 0 in ts:
                sums = work.tile([P, L_TILES], F32, bufs=3)
                exp_tile = work.tile([P, L // RUN, PACK, RUN], F32)
                row_sum[b], exps[b] = sums, exp_tile
            for t in ts:
                nc.scalar.activation(
                    out=exps[b][:, :, t, :],
                    in_=rows_banks[b, t][:].rearrange("p (c i) -> p c i", i=RUN),
                    func=ACT.Exp,
                    bias=neg_max[b][:, t : t + 1],
                    scale=1.0,
                    accum_out=row_sum[b][:, t : t + 1],
                )

        inv_sums = {}

        def recip(b):
            inv_sum = work.tile([P, L_TILES], F32, bufs=3)
            nc.vector.reciprocal(out=inv_sum[:], in_=row_sum[b][:])
            inv_sums[b] = inv_sum
            att_group = work.tile([P, L, PACK], BF16, align_bytes=64)
            att_grouped[b] = att_group

        def norm_part(engine, inv, b, lo, hi):
            engine.tensor_tensor(
                out=att_grouped[b][:, lo:hi, :].rearrange("p (c i) t -> p c t i", i=RUN),
                in0=exps[b][:, lo // RUN : hi // RUN, :, :],
                in1=inv[:].unsqueeze(1).unsqueeze(3).to_broadcast([P, (hi - lo) // RUN, PACK, RUN]),
                op=ALU.mult,
            )

        def normalise_first(b):
            norm_part(nc.gpsimd, inv_sums[b], b, 0, G_COLUMNS if b < B - 2 else LATE_COLUMNS)

        def normalise_rest(b):
            norm_part(nc.vector, inv_sums[b], b, G_COLUMNS if b < B - 2 else LATE_COLUMNS, L)

        def normalise_last():
            b = B - 1
            for t in range(PACK):
                nc.scalar.activation(
                    out=att_grouped[b][:, LATE_COLUMNS:, t].rearrange("p (c i) -> p c i", i=RUN),
                    in_=exps[b][:, LATE_COLUMNS // RUN :, t, :],
                    func=ACT.Copy,
                    scale=inv_sums[b][:, t : t + 1],
                )
            norm_part(nc.vector, inv_sums[b], b, 0, LATE_COLUMNS)

        def quantise_att(b):
            att_codes = work.tile([P, L], U32, align_bytes=64)
            att_scales = work.tile([P, L], U8, align_bytes=64)
            nc.vector.quantize_mx(
                out=att_codes[:].bitcast(FP8X4),
                scales=att_scales[:],
                in_=att_grouped[b][:].rearrange("p m t -> p (m t)"),
            )
            att_mx[b] = (att_codes, att_scales)

        def second_matmul(b, *tiles):
            att_codes, att_scales = att_mx[b]
            v_codes, v_scales = v_mx[b]
            for i in tiles:
                o = psum.tile([P, L], F32, tag="o%d" % i)
                nc.tensor.matmul_mx(
                    out=o[:],
                    lhsT=v_codes[:, i * P : (i + 1) * P].bitcast(FP8X4),
                    lhsT_scale=v_scales[:, i * P : (i + 1) * P],
                    rhs=att_codes[:].bitcast(FP8X4),
                    rhs_scale=att_scales[:],
                    start=True,
                    stop=True,
                )
                o_banks[b, i] = o

        results = {}

        def gain_and_residual(b, *tiles):
            if 0 in tiles:
                result = work.tile([P, D_TILES, L], F32, bufs=3)
                results[b] = result
            result = results[b]
            out_rows = out[b].rearrange("(i p h) j -> p i (h j)", i=D_TILES, h=2)
            for i in tiles:
                nc.vector.scalar_tensor_tensor(
                    out=result[:, i, :],
                    in0=o_banks[b, i][:],
                    scalar=gamma[:, 0:1],
                    in1=x_rows[b][:, i, :],
                    op0=ALU.mult,
                    op1=ALU.add,
                )
                nc.sync.dma_start(out=out_rows[:, i, :], in_=result[:, i, :])

        def do(stage, b, *args):
            if 0 <= b < B:
                stage(b, *args)

        zeros = const.tile([P, L], BF16)
        nc.vector.memset(zeros[:], 0.0)

        def wake(n):
            for i in range(n):
                unread = psum.tile([P, L], F32, tag="o1")
                nc.tensor.matmul(out=unread[:], lhsT=zeros[:, 0:P], rhs=zeros[:], start=True, stop=True)

        bias_rows = const.tile([P, P], F32)
        nc.scalar.copy(out=bias_rows[:], in_=bias_rows_bf[:])
        wake(4)
        turn_energy(0, 0)
        turn_energy(0, 1)
        wake(2)
        empty_energy(0, 0, True)
        empty_energy(0, 1)
        w_grouped = const.tile([P, PACK * L], BF16, align_bytes=64)
        w0 = turn_bank(nc, psum, identity[:], w_rows[:], 0, "rows0")
        w1 = turn_bank(nc, psum, identity[:], w_rows[:], 1, "rows1")
        bias_turned = psum.tile([P, P], F32, tag="o0")
        nc.tensor.transpose(bias_turned[:], bias_rows[:], identity[:])
        wake(2)
        turn_energy(1, 0)
        turn_energy(1, 1)
        wake(3)
        empty_bank(w0, w_grouped[:], 0, nc.scalar.copy)
        empty_bank(w1, w_grouped[:], 1, nc.vector.tensor_copy)
        quantise_energy(0)
        bias_col = const.tile([P, L_TILES], F32)
        nc.scalar.copy(out=bias_col[:], in_=bias_turned[:, 0:L_TILES])
        w_codes = const.tile([P, L], U32, align_bytes=64)
        w_scales = const.tile([P, L], U8, align_bytes=64)
        nc.vector.quantize_mx(out=w_codes[:].bitcast(FP8X4), scales=w_scales[:], in_=w_grouped[:])
        gamma = const.tile([P, 1], F32)
        nc.scalar.copy(out=gamma[:], in_=gamma_bf[:])
        first_matmul(0, 0, 1, 2, 3)
        empty_energy(1, 0)
        empty_energy(1, 1)
        add_bias(0, 0, 2)
        add_bias_v(0, 1, 3)
        quantise_energy(1)
        turn_logits(0, 0, 1)
        turn_energy(2, 0)
        turn_energy(2, 1)
        first_matmul(1, 0, 1)
        regroup_v2(0)
        row_max(0, 0, 1)
        exponentials(0, 0, 1)
        empty_energy(2, 0)
        empty_energy(2, 1)
        for s in range(B):
            do(add_bias, s + 1, 0, 1)
            if s > 0:
                do(turn_logits, s, 0, 1)
                do(row_max, s, 0, 1)
                do(exponentials, s, 0, 1)
            do(second_matmul, s - 2, 0, 1)
            do(first_matmul, s + 1, 2, 3)
            do(gain_and_residual, s - 2, 0, 1)
            do(add_bias, s + 1, 2, 3)
            do(turn_logits, s, 2, 3)
            do(row_max, s, 2, 3)
            do(exponentials, s, 2, 3)
            do(keep_warm, min(s + 1, B - 1), "turned%d")
            do(turn_energy, s + 3, 0)
            do(turn_energy, s + 3, 1)
            do(keep_warm, min(s + 1, B - 1), "z%d")
            do(normalise_rest, s - 1)
            do(quantise_energy, s + 2)
            do(quantise_att, s - 1)
            do(recip, s)
            do(quantise_v2, s)
            do(first_matmul, s + 2, 0, 1)
            do(normalise_first, s) if s < B - 1 else normalise_last()
            do(empty_energy, s + 3, 0)
            do(empty_energy, s + 3, 1)
            do(regroup_v2, s + 1)
        second_matmul(B - 2, 0, 1)
        gain_and_residual(B - 2, 0)
        quantise_att(B - 1)
        second_matmul(B - 1, 0)
        gain_and_residual(B - 2, 1)
        second_matmul(B - 1, 1)
        gain_and_residual(B - 1, 0, 1)
